import numpy as np
import ml_dtypes


def mxq(x, axis, fmt="e4m3"):
    dtype, down = {"e4m3": (ml_dtypes.float8_e4m3fn, 7), "e5m2": (ml_dtypes.float8_e5m2, 14)}[fmt]
    v = np.moveaxis(np.asarray(x, np.float32).astype(ml_dtypes.bfloat16).astype(np.float64), axis, -1)
    blocks = v.reshape(v.shape[:-1] + (-1, 32))
    amax = np.abs(blocks).max(-1, keepdims=True)
    byte = np.maximum(np.where(amax > 0, np.frexp(amax)[1] - 1 + 127, 0) - down, 1)
    scale = np.exp2(byte - 127.0)
    codes = (blocks / scale).astype(np.float32).astype(dtype).astype(np.float64)
    return np.moveaxis((codes * scale).reshape(v.shape), -1, axis)


WIDE = False


def mx_kscale(k):
    if not WIDE:
        return np.ones(k)
    levels = np.array([10, -10, 5, -5, 0])
    if k % 512:
        return np.exp2(np.random.permutation(np.resize(levels, k // 32))).repeat(32)
    a = np.empty((k // 512, 16))
    for p in range(k // 512):
        a[p, :8] = np.random.permutation(np.resize(levels, 8))
        for g in range(8):
            far = levels[np.abs(levels - a[p, g]) >= 10]
            a[p, g + 8] = far[np.random.randint(len(far))]
    return np.exp2(a.ravel()).repeat(32)


BF16 = ml_dtypes.bfloat16


def bf(x):
    return np.asarray(x, np.float32).astype(BF16)


def f64(x):
    return np.asarray(x).astype(np.float64)


E2M1 = np.array([0.0, 0.5, 1.0, 1.5, 2.0, 3.0, 4.0, 6.0, -0.0, -0.5, -1.0, -1.5, -2.0, -3.0, -4.0, -6.0])


def pack_weight(w, fmt):
    k, n = w.shape
    w = f64(bf(w)).reshape(k // 32, 32, n)
    amax = np.abs(w).max(1)
    if fmt == "e4m3":
        byte = np.frexp(amax)[1] - 1 + 127 - 7
    else:
        mant, ex = np.frexp(amax / 6.0)
        byte = np.where(mant > 0.5, ex, ex - 1) + 127
    byte = np.clip(np.where(amax > 0, byte, 1), 1, 254)
    scaled = (w * np.exp2(127.0 - byte)[:, None, :]).reshape(k, n).astype(np.float32)
    by_word = np.ascontiguousarray(scaled.reshape(k // 512, 128, 4, n).transpose(0, 1, 3, 2))
    if fmt == "e4m3":
        words = by_word.astype(ml_dtypes.float8_e4m3fn).view(np.uint8)
    else:
        c = by_word.astype(ml_dtypes.float4_e2m1fn).view(np.uint8) & 0xF
        words = c[..., 0::2] | (c[..., 1::2] << 4)
    return np.ascontiguousarray(words), np.ascontiguousarray(byte.astype(np.uint8).reshape(k // 512, 16, n))


def unpack_weight(words, scales, fmt):
    g, p, n, _ = words.shape
    if fmt == "e4m3":
        vals = np.ascontiguousarray(words).view(ml_dtypes.float8_e4m3fn).astype(np.float64)
    else:
        nib = np.empty((g, p, n, 4), np.uint8)
        nib[..., 0::2] = words & 0xF
        nib[..., 1::2] = words >> 4
        vals = E2M1[nib]
    vals = vals * np.repeat(np.exp2(scales.astype(np.float64) - 127.0), 8, axis=1)[..., None]
    return vals.transpose(0, 1, 3, 2).reshape(g * 512, n)


B, L, E, H, DH, RK, RD, MAXLEN = 4, 1024, 512, 4, 64, 512, 128, 4096


def apply_rope(x, cos, sin):
    cos = cos[None, :, None, :]
    sin = sin[None, :, None, :]
    x1, x2 = x[..., 0::2], x[..., 1::2]
    out_real = x1 * cos - x2 * sin
    out_imag = x1 * sin + x2 * cos
    return np.stack([out_real, out_imag], axis=-1).reshape(x.shape)


def draw0():
    s, t = mx_kscale(E), mx_kscale(RK)
    tc = np.concatenate([t, np.ones(RD)])
    x = bf(np.random.standard_normal((B, L, E)) * s)
    cos = bf(np.random.uniform(size=(L, RD // 2)))
    sin = bf(np.random.uniform(size=(L, RD // 2)))
    wkv_down_words, wkv_down_scales = pack_weight(np.random.standard_normal((E, RK + RD)) / np.sqrt(E) / s[:, None] * tc, "e4m3")
    w_up_words, w_up_scales = pack_weight(np.random.standard_normal((RK, H * (2 * DH + RD))) / np.sqrt(RK) / t[:, None], "e4m3")
    return {"x": x,
            "cos": cos,
            "sin": sin,
            "wkv_down_words": wkv_down_words,
            "wkv_down_scales": wkv_down_scales,
            "w_up_words": w_up_words,
            "w_up_scales": w_up_scales}


def core(x, cos, sin, wkv_down_words, wkv_down_scales, w_up_words, w_up_scales):
    kv_lat = mxq(f64(x), 2, "e4m3") @ unpack_weight(wkv_down_words, wkv_down_scales, "e4m3")
    c_kv = kv_lat[..., :RK]
    k_rope = kv_lat[..., RK:]
    k_rope = apply_rope(k_rope[:, :, None, :], f64(cos), f64(sin))[:, :, 0, :]
    up = (mxq(c_kv, 2, "e4m3") @ unpack_weight(w_up_words, w_up_scales, "e4m3")).reshape(B, L, H, 2 * DH + RD)
    k_head = up[..., :DH]
    v_head = up[..., DH:2 * DH]
    v_rope = up[..., 2 * DH:]
    k_rope_b = np.broadcast_to(k_rope[:, :, None, :], (B, L, H, RD))
    k = np.concatenate([k_head, k_rope_b], axis=-1)
    v = np.concatenate([v_head, v_rope], axis=-1)
    return k, v


def e4m3fn_bytes(y):
    return np.clip(np.asarray(y, np.float64), -448.0, 448.0).astype(np.float32).astype(ml_dtypes.float8_e4m3fn).view(np.uint8)


def e4m3fn_values(b):
    return np.asarray(b, np.uint8).view(ml_dtypes.float8_e4m3fn).astype(np.float64)


def setup_inputs():
    d = draw0()
    x0 = np.asarray(d['x']).astype(np.float64)
    s = (np.max(np.abs(x0), axis=(0, 1), keepdims=True) / 448.0).astype(np.float32)
    out = {}
    for k, v in d.items():
        if k == 'x':
            out['x_bytes'] = e4m3fn_bytes(x0 / s.astype(np.float64))
            out['x_scale'] = s
        else:
            out[k] = v
    return out


def reference(x_bytes, x_scale, cos, sin, wkv_down_words, wkv_down_scales, w_up_words, w_up_scales):
    return core(e4m3fn_values(x_bytes) * x_scale.astype(np.float64), cos, sin, wkv_down_words, wkv_down_scales, w_up_words, w_up_scales)

@@ -1,0 +1,310 @@
+from contextlib import ExitStack
+
+import concourse.mybir as mybir
+from concourse.masks import make_identity
+
+F32 = mybir.dt.float32
+BF16 = mybir.dt.bfloat16
+I32 = mybir.dt.int32
+U32 = mybir.dt.uint32
+U8 = mybir.dt.uint8
+FP8 = mybir.dt.float8_e4m3fn
+FP8X4 = mybir.dt.float8_e4m3fn_x4
+MULT = mybir.AluOpType.mult
+ADD = mybir.AluOpType.add
+
+P = 128
+B, L, E, H, DH, RK, RD = 4, 1024, 512, 4, 64, 512, 128
+I = L // P
+DV = DH + RD
+UP = DH + DV
+
+FLOPS = 2 * B * L * E * (RK + RD + H * UP)
+
+
+def tile_multiheadlatentattention_pa_t_w8_kernel(
+    tc, x_bytes, x_scale, cos, sin, wd_words, wd_scales, wu_words, wu_scales, k_out, v_out
+):
+    nc = tc.nc
+    units = [(0, 0, 1), (0, 1, 1)]
+    for b in range(B):
+        for i in range(0, I, 2):
+            if (b, i) not in [(0, 0), (B - 1, I - 2)]:
+                units.append((b, i, 2))
+    units += [(B - 1, I - 2, 1), (B - 1, I - 1, 1)]
+    n_units = len(units)
+
+    with ExitStack() as ctx:
+        keep = ctx.enter_context(tc.tile_pool(name="keep", bufs=1))
+        work = ctx.enter_context(tc.tile_pool(name="work", bufs=3))
+        outs = ctx.enter_context(tc.tile_pool(name="outs", bufs=4))
+        ps_x = ctx.enter_context(tc.psum_pool(name="ps_x", bufs=2))
+        ps_c = ctx.enter_context(tc.psum_pool(name="ps_c", bufs=2))
+        ps_r = ctx.enter_context(tc.psum_pool(name="ps_r", bufs=1))
+        ps_u = ctx.enter_context(tc.psum_pool(name="ps_u", bufs=3))
+
+        wd_s_raw = keep.tile([P, RK + RD], U8, align_bytes=64)
+        wu_s = keep.tile([P, H * UP], U8, align_bytes=64)
+        warm = keep.tile([P, 8], F32)
+        nc.vector.memset(wd_s_raw[:].bitcast(I32), 0)
+        nc.vector.memset(wu_s[:].bitcast(I32), 0)
+        nc.vector.memset(warm[:], 0.0)
+        nc.scalar.copy(out=warm[:, 4:8], in_=warm[:, 0:4])
+        ident = keep.tile([P, P], F32)
+        make_identity(nc, ident[:])
+
+        xb_first = keep.tile([P, 2 * E], U8, align_bytes=64)
+        xb_rest = keep.tile([P, (I - 2) * E], U8, align_bytes=64)
+        xb_1 = keep.tile([P, I * E], U8, align_bytes=64)
+        xb_2 = keep.tile([P, I * E], U8, align_bytes=64)
+        xb_3 = keep.tile([P, I * E], U8, align_bytes=64)
+        xsc = keep.tile([P, 2, 2], F32)
+        wd_raw = keep.tile([P, RK], U32, align_bytes=64)
+        wd = keep.tile([P, RK], U32, align_bytes=64)
+        wd_s = keep.tile([P, RK], U8, align_bytes=64)
+        wr = keep.tile([P, 2 * RD], U32, align_bytes=64)
+        wr_s = keep.tile([P, 2 * RD], U8, align_bytes=64)
+        wu = keep.tile([P, H * UP], U32, align_bytes=64)
+        cos_sb = keep.tile([P, I, RD // 2], BF16)
+        sin_sb = keep.tile([P, I, RD // 2], BF16)
+        tab = keep.tile([P, I, 2, RD], BF16)
+
+        xv = [x_bytes[b].rearrange("(p i) k -> p (i k)", i=I) for b in range(B)]
+        wdw = wd_words[0].rearrange("p n t -> p (n t)").bitcast(I32)
+        wuw = wu_words[0].rearrange("p n t -> p (n t)").bitcast(I32)
+        nc.sync.dma_start(out=xb_first[:], in_=xv[0][:, 0 : 2 * E])
+        nc.sync.dma_start(out=wd_raw[:].bitcast(I32), in_=wdw[:, 0:RK])
+        for q in range(4):
+            nc.sync.dma_start(
+                out=wd_s_raw[32 * q : 32 * q + 4, :].bitcast(I32), in_=wd_scales[0, 4 * q : 4 * q + 4, :].bitcast(I32)
+            )
+        nc.sync.dma_start(out=xsc[:], in_=x_scale.rearrange("a b (p u e) -> p (a b u) e", u=2, e=2))
+        nc.sync.dma_start(out=xb_rest[:], in_=xv[0][:, 2 * E :])
+        nc.sync.dma_start(out=wu[:].bitcast(I32), in_=wuw)
+        nc.sync.dma_start(out=wr[:, 0:RD].bitcast(I32), in_=wdw[:, RK:])
+        for q in range(4):
+            nc.sync.dma_start(
+                out=wu_s[32 * q : 32 * q + 4, :].bitcast(I32), in_=wu_scales[0, 4 * q : 4 * q + 4, :].bitcast(I32)
+            )
+        nc.sync.dma_start(out=cos_sb[:], in_=cos.rearrange("(p i) j -> p i j", i=I))
+        nc.sync.dma_start(out=sin_sb[:], in_=sin.rearrange("(p i) j -> p i j", i=I))
+        nc.sync.dma_start(out=xb_1[:], in_=xv[1])
+        nc.sync.dma_start(out=xb_2[:], in_=xv[2])
+        nc.sync.dma_start(out=xb_3[:], in_=xv[3])
+
+        nc.vector.tensor_copy(
+            out=wd[:].bitcast(I32).rearrange("p (t m) -> p t m", t=4),
+            in_=wd_raw[:].bitcast(I32).rearrange("p (m t) -> p t m", t=4),
+        )
+        nc.vector.tensor_copy(
+            out=wd_s[:].rearrange("p (t m) -> p t m", t=4), in_=wd_s_raw[:, 0:RK].rearrange("p (m t) -> p t m", t=4)
+        )
+        nc.gpsimd.tensor_copy(out=wr_s[:, 0:RD], in_=wd_s_raw[:, RK:])
+        rs_src = wd_s_raw[:, RK:].rearrange("p (j e) -> p j e", e=2)
+        rs_dst = wr_s[:, RD:].rearrange("p (j e) -> p j e", e=2)
+        for e in range(2):
+            nc.gpsimd.tensor_copy(out=rs_dst[:, :, e], in_=rs_src[:, :, 1 - e])
+        tabv = tab[:].rearrange("p i g (j e) -> p i g j e", e=2)
+        for e in range(2):
+            nc.gpsimd.tensor_scalar(
+                out=tabv[:, :, 0, :, e], in0=cos_sb[:], scalar1=1.0, scalar2=0.0, op0=MULT, op1=ADD
+            )
+            nc.gpsimd.tensor_scalar(
+                out=tabv[:, :, 1, :, e], in0=sin_sb[:], scalar1=(2.0 * e - 1.0), scalar2=0.0, op0=MULT, op1=ADD
+            )
+
+        xw, xt, xg, xq, xs, pc, cg, cq, cs, pr, ab, kt, vt = [{} for j in range(13)]
+
+        def x_source(n):
+            b, i, w = units[n]
+            if b == 0:
+                return xb_first[:, i * E : (i + w) * E] if i < 2 else xb_rest[:, (i - 2) * E : (i - 2 + w) * E]
+            return [xb_1, xb_2, xb_3][b - 1][:, i * E : (i + w) * E]
+
+        def widen(n):
+            w = units[n][2]
+            xw[n] = work.tile([P, 2 * E], BF16, name="xw")
+            if n < 2:
+                nc.scalar.copy(out=xw[n][:, 0 : w * E], in_=x_source(n).bitcast(FP8))
+            else:
+                nc.vector.tensor_copy(out=xw[n][:, 0 : w * E], in_=x_source(n).bitcast(FP8))
+
+        def turn(n):
+            w = units[n][2]
+            xt[n] = ps_x.tile([P, 2, 2 * P], F32, name="xt")
+            words = xw[n][:].bitcast(F32)
+            for j in range(w):
+                for u in range(2):
+                    nc.tensor.transpose(
+                        xt[n][:, u, j * P : (j + 1) * P], words[:, j * 256 + u : (j + 1) * 256 : 2], ident[:]
+                    )
+
+        def scale_x(n):
+            r = units[n][2] * P
+            xg[n] = work.tile([P, 2 * P, 4], BF16, name="xg", align_bytes=64)
+            nc.vector.tensor_tensor(
+                out=xg[n][:, 0:r, :].rearrange("p r (u e) -> p r u e", e=2),
+                in0=xt[n][:].bitcast(BF16).rearrange("p u (r e) -> p r u e", e=2)[:, 0:r],
+                in1=xsc[:].unsqueeze(1).to_broadcast([P, r, 2, 2]),
+                op=MULT,
+            )
+
+        def quant_x(n):
+            r = units[n][2] * P
+            xq[n] = work.tile([P, 2 * P], U32, name="xq", align_bytes=64)
+            xs[n] = work.tile([P, 2 * P], U8, name="xs", align_bytes=64)
+            nc.vector.quantize_mx(
+                out=xq[n][:, 0:r].bitcast(FP8X4),
+                scales=xs[n][:, 0:r],
+                in_=xg[n][:, 0:r, :].rearrange("p r t -> p (r t)"),
+            )
+
+        def latent(n):
+            pc[n] = []
+            for j in range(units[n][2]):
+                acc = ps_c.tile([P, 4, P], F32, name="pc")
+                pc[n].append(acc)
+                for t in range(4):
+                    nc.tensor.matmul_mx(
+                        out=acc[:, t, :],
+                        lhsT=wd[:, t * P : (t + 1) * P].bitcast(FP8X4),
+                        lhsT_scale=wd_s[:, t * P : (t + 1) * P],
+                        rhs=xq[n][:, j * P : (j + 1) * P].bitcast(FP8X4),
+                        rhs_scale=xs[n][:, j * P : (j + 1) * P],
+                        start=True,
+                        stop=True,
+                    )
+
+        def rope_key(n):
+            pr[n] = ps_r.tile([P, 2, 2 * RD], F32, name="pr")
+            for j in range(units[n][2]):
+                nc.tensor.matmul_mx(
+                    out=pr[n][:, j, :],
+                    lhsT=xq[n][:, j * P : (j + 1) * P].bitcast(FP8X4),
+                    lhsT_scale=xs[n][:, j * P : (j + 1) * P],
+                    rhs=wr[:].bitcast(FP8X4),
+                    rhs_scale=wr_s[:],
+                    start=True,
+                    stop=True,
+                )
+
+        def latent_out(n):
+            cg[n] = work.tile([P, 2 * P, 4], BF16, name="cg", align_bytes=64)
+            for j in range(units[n][2]):
+                nc.scalar.copy(out=cg[n][:, j * P : (j + 1) * P, :], in_=pc[n][j][:].rearrange("p t r -> p r t"))
+
+        def quant_c(n):
+            r = units[n][2] * P
+            cq[n] = work.tile([P, 2 * P], U32, name="cq", align_bytes=64)
+            cs[n] = work.tile([P, 2 * P], U8, name="cs", align_bytes=64)
+            nc.vector.quantize_mx(
+                out=cq[n][:, 0:r].bitcast(FP8X4),
+                scales=cs[n][:, 0:r],
+                in_=cg[n][:, 0:r, :].rearrange("p r t -> p (r t)"),
+            )
+
+        def rotate(n):
+            b, i, w = units[n]
+            ab[n] = work.tile([P, 2, 2, RD], F32, name="ab")
+            nc.vector.tensor_tensor(
+                out=ab[n][:, 0:w],
+                in0=pr[n][:, 0:w, :].rearrange("p w (g c) -> p w g c", g=2),
+                in1=tab[:, i : i + w],
+                op=MULT,
+            )
+
+        def rotate_sum(n):
+            w = units[n][2]
+            nc.vector.tensor_tensor(
+                out=kt[n][:, 0:w, 0, DH:], in0=ab[n][:, 0:w, 0, :], in1=ab[n][:, 0:w, 1, :], op=ADD
+            )
+
+        def spread(n):
+            w = units[n][2]
+            nc.gpsimd.tensor_scalar(
+                out=kt[n][:, 0:w, 1:, DH:],
+                in0=kt[n][:, 0:w, 0:1, DH:].to_broadcast([P, w, H - 1, RD]),
+                scalar1=1.0,
+                scalar2=0.0,
+                op0=MULT,
+                op1=ADD,
+            )
+
+        def new_out(n):
+            kt[n] = outs.tile([P, 2, H, DV], F32, name="kt")
+            vt[n] = outs.tile([P, 2, H, DV], F32, name="vt")
+
+        def expand(n, j):
+            accs = []
+            for g in range(2):
+                acc = ps_u.tile([P, 2, UP], F32, name="pu")
+                accs.append(acc)
+                cols = slice(g * 2 * UP, (g + 1) * 2 * UP)
+                nc.tensor.matmul_mx(
+                    out=acc[:].rearrange("p h c -> p (h c)"),
+                    lhsT=cq[n][:, j * P : (j + 1) * P].bitcast(FP8X4),
+                    lhsT_scale=cs[n][:, j * P : (j + 1) * P],
+                    rhs=wu[:, cols].bitcast(FP8X4),
+                    rhs_scale=wu_s[:, cols],
+                    start=True,
+                    stop=True,
+                )
+            return accs
+
+        def expand_out(n, j, accs):
+            for g in range(2):
+                v_copy = nc.vector.tensor_copy if n < 2 and g == 1 else nc.scalar.copy
+                k_copy = nc.vector.tensor_copy if g == 1 and j == 0 else nc.scalar.copy
+                v_copy(out=vt[n][:, j, 2 * g : 2 * g + 2, :], in_=accs[g][:, :, DH:])
+                k_copy(out=kt[n][:, j, 2 * g : 2 * g + 2, 0:DH], in_=accs[g][:, :, 0:DH])
+
+        def store(n):
+            b, i, w = units[n]
+            for hbm, sb in ((v_out, vt[n]), (k_out, kt[n])):
+                nc.sync.dma_start(
+                    out=hbm[b].rearrange("(p i) h d -> p i (h d)", i=I)[:, i : i + w, :],
+                    in_=sb[:, 0:w].rearrange("p w h d -> p w (h d)"),
+                )
+
+        widen(0)
+        widen(1)
+        turn(0)
+        turn(1)
+        scale_x(0)
+        rw_src = wr[:, 0:RD].bitcast(I32).rearrange("p (j e) -> p j e", e=2)
+        rw_dst = wr[:, RD:].bitcast(I32).rearrange("p (j e) -> p j e", e=2)
+        quant_x(0)
+        latent(0)
+        latent_out(0)
+        for n in range(n_units):
+            first = n == 0
+            new_out(n)
+            if n + 1 < n_units:
+                scale_x(n + 1)
+            if n + 2 < n_units:
+                widen(n + 2)
+                turn(n + 2)
+            if first:
+                for e in range(2):
+                    nc.gpsimd.tensor_copy(out=rw_dst[:, :, e], in_=rw_src[:, :, 1 - e])
+            quant_c(n)
+            if not first:
+                rotate(n)
+            if n + 1 < n_units:
+                quant_x(n + 1)
+            accs = expand(n, 0)
+            expand_out(n, 0, accs)
+            if units[n][2] == 2:
+                accs = expand(n, 1)
+            if first:
+                rope_key(0)
+                rotate(0)
+            if n + 1 < n_units:
+                latent(n + 1)
+                rope_key(n + 1)
+                latent_out(n + 1)
+            if units[n][2] == 2:
+                expand_out(n, 1, accs)
+            rotate_sum(n)
+            spread(n)
+            store(n)

@@ -26,108 +26,103 @@ def tile_multiheadlatentattention_pa_t_w8_kernel(
     tc, x_bytes, x_scale, cos, sin, wd_words, wd_scales, wu_words, wu_scales, k_out, v_out
 ):
     nc = tc.nc
-    units = [(0, 0, 1), (0, 1, 1)]
-    for b in range(B):
-        for i in range(0, I, 2):
-            if (b, i) not in [(0, 0), (B - 1, I - 2)]:
-                units.append((b, i, 2))
-    units += [(B - 1, I - 2, 1), (B - 1, I - 1, 1)]
-    n_units = len(units)
+    tiles = [(b, i) for b in range(B) for i in range(I)]
+    units = []
+    while tiles:
+        width = 1 if len(units) < 4 or len(tiles) <= 2 else 2
+        units.append((tiles[0][0], tiles[0][1], width))
+        tiles = tiles[width:]
+    last = len(units) - 1
 
     with ExitStack() as ctx:
         keep = ctx.enter_context(tc.tile_pool(name="keep", bufs=1))
         work = ctx.enter_context(tc.tile_pool(name="work", bufs=3))
-        outs = ctx.enter_context(tc.tile_pool(name="outs", bufs=4))
+        outs = ctx.enter_context(tc.tile_pool(name="outs", bufs=5))
         ps_x = ctx.enter_context(tc.psum_pool(name="ps_x", bufs=2))
         ps_c = ctx.enter_context(tc.psum_pool(name="ps_c", bufs=2))
         ps_r = ctx.enter_context(tc.psum_pool(name="ps_r", bufs=1))
         ps_u = ctx.enter_context(tc.psum_pool(name="ps_u", bufs=3))
+        ctx.enter_context(tc.manual_schedule())
 
-        wd_s_raw = keep.tile([P, RK + RD], U8, align_bytes=64)
+        wd_raw = keep.tile([P, RK + 2 * RD], U32, align_bytes=64)
+        wd_s_raw = keep.tile([P, RK + 2 * RD], U8, align_bytes=64)
+        wd = keep.tile([P, RK], U32, align_bytes=64)
+        wd_s = keep.tile([P, RK], U8, align_bytes=64)
+        wu = keep.tile([P, H * UP], U32, align_bytes=64)
         wu_s = keep.tile([P, H * UP], U8, align_bytes=64)
-        warm = keep.tile([P, 8], F32)
-        nc.vector.memset(wd_s_raw[:].bitcast(I32), 0)
-        nc.vector.memset(wu_s[:].bitcast(I32), 0)
-        nc.vector.memset(warm[:], 0.0)
-        nc.scalar.copy(out=warm[:, 4:8], in_=warm[:, 0:4])
-        ident = keep.tile([P, P], F32)
-        make_identity(nc, ident[:])
-
         xb_first = keep.tile([P, 2 * E], U8, align_bytes=64)
         xb_rest = keep.tile([P, (I - 2) * E], U8, align_bytes=64)
         xb_1 = keep.tile([P, I * E], U8, align_bytes=64)
         xb_2 = keep.tile([P, I * E], U8, align_bytes=64)
         xb_3 = keep.tile([P, I * E], U8, align_bytes=64)
         xsc = keep.tile([P, 2, 2], F32)
-        wd_raw = keep.tile([P, RK], U32, align_bytes=64)
-        wd = keep.tile([P, RK], U32, align_bytes=64)
-        wd_s = keep.tile([P, RK], U8, align_bytes=64)
-        wr = keep.tile([P, 2 * RD], U32, align_bytes=64)
-        wr_s = keep.tile([P, 2 * RD], U8, align_bytes=64)
-        wu = keep.tile([P, H * UP], U32, align_bytes=64)
         cos_sb = keep.tile([P, I, RD // 2], BF16)
         sin_sb = keep.tile([P, I, RD // 2], BF16)
-        tab = keep.tile([P, I, 2, RD], BF16)
+        tab_a = keep.tile([P, I // 2, 2, RD], BF16)
+        tab_b = keep.tile([P, I // 2, 2, RD], BF16)
+        ident = keep.tile([P, P], F32)
+        warm = keep.tile([P, 8], F32)
 
+        nc.vector.memset(wd_s_raw[:].bitcast(I32), 0)
+        nc.vector.memset(wu_s[:].bitcast(I32), 0)
+        nc.vector.memset(warm[:], 0.0)
+        nc.scalar.copy(out=warm[:, 4:8], in_=warm[:, 0:4])
+        make_identity(nc, ident[:])
+        nc.gpsimd.dma_start(out=xsc[:], in_=x_scale.rearrange("a b (p u e) -> p (a b u) e", u=2, e=2))
+        nc.gpsimd.dma_start(out=cos_sb[:], in_=cos.rearrange("(p i) j -> p i j", i=I))
+        nc.gpsimd.dma_start(out=sin_sb[:], in_=sin.rearrange("(p i) j -> p i j", i=I))
         xv = [x_bytes[b].rearrange("(p i) k -> p (i k)", i=I) for b in range(B)]
-        wdw = wd_words[0].rearrange("p n t -> p (n t)").bitcast(I32)
-        wuw = wu_words[0].rearrange("p n t -> p (n t)").bitcast(I32)
         nc.sync.dma_start(out=xb_first[:], in_=xv[0][:, 0 : 2 * E])
-        nc.sync.dma_start(out=wd_raw[:].bitcast(I32), in_=wdw[:, 0:RK])
+        nc.sync.dma_start(
+            out=wd_raw[:, 0 : RK + RD].bitcast(I32), in_=wd_words[0].rearrange("p n t -> p (n t)").bitcast(I32)
+        )
         for q in range(4):
             nc.sync.dma_start(
-                out=wd_s_raw[32 * q : 32 * q + 4, :].bitcast(I32), in_=wd_scales[0, 4 * q : 4 * q + 4, :].bitcast(I32)
+                out=wd_s_raw[32 * q : 32 * q + 4, 0 : RK + RD].bitcast(I32),
+                in_=wd_scales[0, 4 * q : 4 * q + 4, :].bitcast(I32),
             )
-        nc.sync.dma_start(out=xsc[:], in_=x_scale.rearrange("a b (p u e) -> p (a b u) e", u=2, e=2))
         nc.sync.dma_start(out=xb_rest[:], in_=xv[0][:, 2 * E :])
-        nc.sync.dma_start(out=wu[:].bitcast(I32), in_=wuw)
-        nc.sync.dma_start(out=wr[:, 0:RD].bitcast(I32), in_=wdw[:, RK:])
+        nc.sync.dma_start(out=wu[:].bitcast(I32), in_=wu_words[0].rearrange("p n t -> p (n t)").bitcast(I32))
         for q in range(4):
             nc.sync.dma_start(
                 out=wu_s[32 * q : 32 * q + 4, :].bitcast(I32), in_=wu_scales[0, 4 * q : 4 * q + 4, :].bitcast(I32)
             )
-        nc.sync.dma_start(out=cos_sb[:], in_=cos.rearrange("(p i) j -> p i j", i=I))
-        nc.sync.dma_start(out=sin_sb[:], in_=sin.rearrange("(p i) j -> p i j", i=I))
         nc.sync.dma_start(out=xb_1[:], in_=xv[1])
         nc.sync.dma_start(out=xb_2[:], in_=xv[2])
         nc.sync.dma_start(out=xb_3[:], in_=xv[3])
 
-        nc.vector.tensor_copy(
-            out=wd[:].bitcast(I32).rearrange("p (t m) -> p t m", t=4),
-            in_=wd_raw[:].bitcast(I32).rearrange("p (m t) -> p t m", t=4),
-        )
-        nc.vector.tensor_copy(
-            out=wd_s[:].rearrange("p (t m) -> p t m", t=4), in_=wd_s_raw[:, 0:RK].rearrange("p (m t) -> p t m", t=4)
-        )
-        nc.gpsimd.tensor_copy(out=wr_s[:, 0:RD], in_=wd_s_raw[:, RK:])
-        rs_src = wd_s_raw[:, RK:].rearrange("p (j e) -> p j e", e=2)
-        rs_dst = wr_s[:, RD:].rearrange("p (j e) -> p j e", e=2)
-        for e in range(2):
-            nc.gpsimd.tensor_copy(out=rs_dst[:, :, e], in_=rs_src[:, :, 1 - e])
-        tabv = tab[:].rearrange("p i g (j e) -> p i g j e", e=2)
-        for e in range(2):
-            nc.gpsimd.tensor_scalar(
-                out=tabv[:, :, 0, :, e], in0=cos_sb[:], scalar1=1.0, scalar2=0.0, op0=MULT, op1=ADD
-            )
-            nc.gpsimd.tensor_scalar(
-                out=tabv[:, :, 1, :, e], in0=sin_sb[:], scalar1=(2.0 * e - 1.0), scalar2=0.0, op0=MULT, op1=ADD
+        def tables(tab, i0):
+            view = tab[:].rearrange("p i g (j e) -> p i g j e", e=2)
+            for g, src in ((0, cos_sb), (1, sin_sb)):
+                for e in range(2):
+                    factor = -1.0 if (g, e) == (1, 0) else 1.0
+                    nc.gpsimd.tensor_scalar(
+                        out=view[:, :, g, :, e],
+                        in0=src[:, i0 : i0 + I // 2, :],
+                        scalar1=factor,
+                        scalar2=0.0,
+                        op0=MULT,
+                        op1=ADD,
+                    )
+
+        def permute(dst, src):
+            nc.vector.tensor_copy(
+                out=dst.rearrange("p (t m) -> p t m", t=4), in_=src.rearrange("p (m t) -> p t m", t=4)
             )
 
-        xw, xt, xg, xq, xs, pc, cg, cq, cs, pr, ab, kt, vt = [{} for j in range(13)]
+        xw, xt, xg, xq, xs, pc, cg, cq, cs, pr, ab, kt, vt, pu = [{} for j in range(14)]
 
         def x_source(n):
             b, i, w = units[n]
-            if b == 0:
-                return xb_first[:, i * E : (i + w) * E] if i < 2 else xb_rest[:, (i - 2) * E : (i - 2 + w) * E]
-            return [xb_1, xb_2, xb_3][b - 1][:, i * E : (i + w) * E]
+            if b > 0:
+                return [xb_1, xb_2, xb_3][b - 1][:, i * E : (i + w) * E]
+            return xb_first[:, i * E : (i + w) * E] if i < 2 else xb_rest[:, (i - 2) * E : (i - 2 + w) * E]
 
         def widen(n):
             w = units[n][2]
-            xw[n] = work.tile([P, 2 * E], BF16, name="xw")
-            if n < 2:
-                nc.scalar.copy(out=xw[n][:, 0 : w * E], in_=x_source(n).bitcast(FP8))
-            else:
-                nc.vector.tensor_copy(out=xw[n][:, 0 : w * E], in_=x_source(n).bitcast(FP8))
+            xw[n] = work.tile([P, 2 * E], BF16, name="xw", bufs=4)
+            copy = nc.scalar.copy if n in (1, 2, 3) else nc.vector.tensor_copy
+            copy(out=xw[n][:, 0 : w * E], in_=x_source(n).bitcast(FP8))
 
         def turn(n):
             w = units[n][2]
@@ -182,8 +177,8 @@ def tile_multiheadlatentattention_pa_t_w8_kernel(
                     out=pr[n][:, j, :],
                     lhsT=xq[n][:, j * P : (j + 1) * P].bitcast(FP8X4),
                     lhsT_scale=xs[n][:, j * P : (j + 1) * P],
-                    rhs=wr[:].bitcast(FP8X4),
-                    rhs_scale=wr_s[:],
+                    rhs=wd_raw[:, RK:].bitcast(FP8X4),
+                    rhs_scale=wd_s_raw[:, RK:],
                     start=True,
                     stop=True,
                 )
@@ -205,11 +200,12 @@ def tile_multiheadlatentattention_pa_t_w8_kernel(
 
         def rotate(n):
             b, i, w = units[n]
+            tab, i0 = (tab_a, 0) if i < I // 2 else (tab_b, I // 2)
             ab[n] = work.tile([P, 2, 2, RD], F32, name="ab")
             nc.vector.tensor_tensor(
                 out=ab[n][:, 0:w],
                 in0=pr[n][:, 0:w, :].rearrange("p w (g c) -> p w g c", g=2),
-                in1=tab[:, i : i + w],
+                in1=tab[:, i - i0 : i - i0 + w],
                 op=MULT,
             )
 
@@ -221,24 +217,21 @@ def tile_multiheadlatentattention_pa_t_w8_kernel(
 
         def spread(n):
             w = units[n][2]
-            nc.gpsimd.tensor_scalar(
-                out=kt[n][:, 0:w, 1:, DH:],
-                in0=kt[n][:, 0:w, 0:1, DH:].to_broadcast([P, w, H - 1, RD]),
-                scalar1=1.0,
-                scalar2=0.0,
-                op0=MULT,
-                op1=ADD,
-            )
+            out = kt[n][:, 0:w, 1:, DH:]
+            src = kt[n][:, 0:w, 0:1, DH:].to_broadcast([P, w, H - 1, RD])
+            if n == last:
+                nc.vector.tensor_copy(out=out, in_=src)
+            else:
+                nc.gpsimd.tensor_scalar(out=out, in0=src, scalar1=1.0, scalar2=0.0, op0=MULT, op1=ADD)
 
         def new_out(n):
             kt[n] = outs.tile([P, 2, H, DV], F32, name="kt")
             vt[n] = outs.tile([P, 2, H, DV], F32, name="vt")
 
         def expand(n, j):
-            accs = []
             for g in range(2):
                 acc = ps_u.tile([P, 2, UP], F32, name="pu")
-                accs.append(acc)
+                pu[n, j, g] = acc
                 cols = slice(g * 2 * UP, (g + 1) * 2 * UP)
                 nc.tensor.matmul_mx(
                     out=acc[:].rearrange("p h c -> p (h c)"),
@@ -249,14 +242,18 @@ def tile_multiheadlatentattention_pa_t_w8_kernel(
                     start=True,
                     stop=True,
                 )
-            return accs
 
-        def expand_out(n, j, accs):
+        def v_out_copy(n, j, g, copy):
+            copy(out=vt[n][:, j, 2 * g : 2 * g + 2, :], in_=pu[n, j, g][:, :, DH:])
+
+        def k_out_copy(n, j, g, copy):
+            copy(out=kt[n][:, j, 2 * g : 2 * g + 2, 0:DH], in_=pu[n, j, g][:, :, 0:DH])
+
+        def expand_out(n, j):
             for g in range(2):
-                v_copy = nc.vector.tensor_copy if n < 2 and g == 1 else nc.scalar.copy
-                k_copy = nc.vector.tensor_copy if g == 1 and j == 0 else nc.scalar.copy
-                v_copy(out=vt[n][:, j, 2 * g : 2 * g + 2, :], in_=accs[g][:, :, DH:])
-                k_copy(out=kt[n][:, j, 2 * g : 2 * g + 2, 0:DH], in_=accs[g][:, :, 0:DH])
+                copy = nc.vector.tensor_copy if n in (0, last) and g == 1 else nc.scalar.copy
+                v_out_copy(n, j, g, copy)
+                k_out_copy(n, j, g, copy)
 
         def store(n):
             b, i, w = units[n]
@@ -266,45 +263,52 @@ def tile_multiheadlatentattention_pa_t_w8_kernel(
                     in_=sb[:, 0:w].rearrange("p w h d -> p w (h d)"),
                 )
 
-        widen(0)
-        widen(1)
-        turn(0)
-        turn(1)
-        scale_x(0)
-        rw_src = wr[:, 0:RD].bitcast(I32).rearrange("p (j e) -> p j e", e=2)
-        rw_dst = wr[:, RD:].bitcast(I32).rearrange("p (j e) -> p j e", e=2)
-        quant_x(0)
-        latent(0)
-        latent_out(0)
-        for n in range(n_units):
-            first = n == 0
-            new_out(n)
-            if n + 1 < n_units:
-                scale_x(n + 1)
-            if n + 2 < n_units:
-                widen(n + 2)
-                turn(n + 2)
-            if first:
-                for e in range(2):
-                    nc.gpsimd.tensor_copy(out=rw_dst[:, :, e], in_=rw_src[:, :, 1 - e])
-            quant_c(n)
-            if not first:
+        src = wd_raw[:, RK : RK + RD].bitcast(I32).rearrange("p (j e) -> p j e", e=2)
+        dst = wd_raw[:, RK + RD :].bitcast(I32).rearrange("p (j e) -> p j e", e=2)
+        src_s = wd_s_raw[:, RK : RK + RD].rearrange("p (j e) -> p j e", e=2)
+        dst_s = wd_s_raw[:, RK + RD :].rearrange("p (j e) -> p j e", e=2)
+        for e in range(2):
+            nc.gpsimd.tensor_copy(out=dst[:, :, e], in_=src[:, :, 1 - e])
+        for e in range(2):
+            nc.gpsimd.tensor_copy(out=dst_s[:, :, e], in_=src_s[:, :, 1 - e])
+        tables(tab_a, 0)
+
+        for m in range(4):
+            widen(m)
+        for n in range(-4, last + 1):
+            if n >= 0:
+                new_out(n)
+                quant_c(n)
+                expand(n, 0)
+                if n + 4 <= last:
+                    widen(n + 4)
                 rotate(n)
-            if n + 1 < n_units:
-                quant_x(n + 1)
-            accs = expand(n, 0)
-            expand_out(n, 0, accs)
-            if units[n][2] == 2:
-                accs = expand(n, 1)
-            if first:
-                rope_key(0)
-                rotate(0)
-            if n + 1 < n_units:
-                latent(n + 1)
+            if n == -3:
+                permute(wd[:].bitcast(I32), wd_raw[:, 0:RK].bitcast(I32))
+            if n == -2:
+                permute(wd_s[:], wd_s_raw[:, 0:RK])
+            if 0 <= n + 2 <= last:
+                quant_x(n + 2)
+            if n >= 0:
+                expand_out(n, 0)
+            if 0 <= n + 2 <= last:
+                latent(n + 2)
+            if n >= 0 and units[n][2] == 2:
+                expand(n, 1)
+            if 0 <= n + 2 <= last:
+                latent_out(n + 2)
+            if 0 <= n + 1 <= last:
                 rope_key(n + 1)
-                latent_out(n + 1)
-            if units[n][2] == 2:
-                expand_out(n, 1, accs)
-            rotate_sum(n)
-            spread(n)
-            store(n)
+            if n + 4 <= last:
+                turn(n + 4)
+            if n >= 0:
+                rotate_sum(n)
+                spread(n)
+            if n == 0:
+                tables(tab_b, I // 2)
+            if 0 <= n + 3 <= last:
+                scale_x(n + 3)
+            if n >= 0:
+                if units[n][2] == 2:
+                    expand_out(n, 1)
+                store(n)

from contextlib import ExitStack

import concourse.mybir as mybir
from concourse.masks import make_identity

F32 = mybir.dt.float32
BF16 = mybir.dt.bfloat16
I32 = mybir.dt.int32
U32 = mybir.dt.uint32
U8 = mybir.dt.uint8
FP8 = mybir.dt.float8_e4m3fn
FP8X4 = mybir.dt.float8_e4m3fn_x4
MULT = mybir.AluOpType.mult
ADD = mybir.AluOpType.add

P = 128
B, L, E, H, DH, RK, RD = 4, 1024, 512, 4, 64, 512, 128
I = L // P
DV = DH + RD
UP = DH + DV

FLOPS = 2 * B * L * E * (RK + RD + H * UP)


def tile_multiheadlatentattention_pa_t_w8_kernel(
    tc, x_bytes, x_scale, cos, sin, wd_words, wd_scales, wu_words, wu_scales, k_out, v_out
):
    nc = tc.nc
    tiles = [(b, i) for b in range(B) for i in range(I)]
    units = []
    while tiles:
        width = 1 if len(units) < 4 or len(tiles) <= 2 else 2
        units.append((tiles[0][0], tiles[0][1], width))
        tiles = tiles[width:]
    last = len(units) - 1

    with ExitStack() as ctx:
        keep = ctx.enter_context(tc.tile_pool(name="keep", bufs=1))
        work = ctx.enter_context(tc.tile_pool(name="work", bufs=3))
        outs = ctx.enter_context(tc.tile_pool(name="outs", bufs=5))
        ps_x = ctx.enter_context(tc.psum_pool(name="ps_x", bufs=2))
        ps_c = ctx.enter_context(tc.psum_pool(name="ps_c", bufs=2))
        ps_r = ctx.enter_context(tc.psum_pool(name="ps_r", bufs=1))
        ps_u = ctx.enter_context(tc.psum_pool(name="ps_u", bufs=3))
        ctx.enter_context(tc.manual_schedule())

        wd_raw = keep.tile([P, RK + 2 * RD], U32, align_bytes=64)
        wd_s_raw = keep.tile([P, RK + 2 * RD], U8, align_bytes=64)
        wd = keep.tile([P, RK], U32, align_bytes=64)
        wd_s = keep.tile([P, RK], U8, align_bytes=64)
        wu = keep.tile([P, H * UP], U32, align_bytes=64)
        wu_s = keep.tile([P, H * UP], U8, align_bytes=64)
        xb_first = keep.tile([P, 2 * E], U8, align_bytes=64)
        xb_rest = keep.tile([P, (I - 2) * E], U8, align_bytes=64)
        xb_1 = keep.tile([P, I * E], U8, align_bytes=64)
        xb_2 = keep.tile([P, I * E], U8, align_bytes=64)
        xb_3 = keep.tile([P, I * E], U8, align_bytes=64)
        xsc = keep.tile([P, 2, 2], F32)
        cos_sb = keep.tile([P, I, RD // 2], BF16)
        sin_sb = keep.tile([P, I, RD // 2], BF16)
        tab_a = keep.tile([P, I // 2, 2, RD], BF16)
        tab_b = keep.tile([P, I // 2, 2, RD], BF16)
        ident = keep.tile([P, P], F32)
        warm = keep.tile([P, 8], F32)

        nc.vector.memset(wd_s_raw[:].bitcast(I32), 0)
        nc.vector.memset(wu_s[:].bitcast(I32), 0)
        nc.vector.memset(warm[:], 0.0)
        nc.scalar.copy(out=warm[:, 4:8], in_=warm[:, 0:4])
        make_identity(nc, ident[:])
        nc.gpsimd.dma_start(out=xsc[:], in_=x_scale.rearrange("a b (p u e) -> p (a b u) e", u=2, e=2))
        nc.gpsimd.dma_start(out=cos_sb[:], in_=cos.rearrange("(p i) j -> p i j", i=I))
        nc.gpsimd.dma_start(out=sin_sb[:], in_=sin.rearrange("(p i) j -> p i j", i=I))
        xv = [x_bytes[b].rearrange("(p i) k -> p (i k)", i=I) for b in range(B)]
        nc.sync.dma_start(out=xb_first[:], in_=xv[0][:, 0 : 2 * E])
        nc.sync.dma_start(
            out=wd_raw[:, 0 : RK + RD].bitcast(I32), in_=wd_words[0].rearrange("p n t -> p (n t)").bitcast(I32)
        )
        for q in range(4):
            nc.sync.dma_start(
                out=wd_s_raw[32 * q : 32 * q + 4, 0 : RK + RD].bitcast(I32),
                in_=wd_scales[0, 4 * q : 4 * q + 4, :].bitcast(I32),
            )
        nc.sync.dma_start(out=xb_rest[:], in_=xv[0][:, 2 * E :])
        nc.sync.dma_start(out=wu[:].bitcast(I32), in_=wu_words[0].rearrange("p n t -> p (n t)").bitcast(I32))
        for q in range(4):
            nc.sync.dma_start(
                out=wu_s[32 * q : 32 * q + 4, :].bitcast(I32), in_=wu_scales[0, 4 * q : 4 * q + 4, :].bitcast(I32)
            )
        nc.sync.dma_start(out=xb_1[:], in_=xv[1])
        nc.sync.dma_start(out=xb_2[:], in_=xv[2])
        nc.sync.dma_start(out=xb_3[:], in_=xv[3])

        def tables(tab, i0):
            view = tab[:].rearrange("p i g (j e) -> p i g j e", e=2)
            for g, src in ((0, cos_sb), (1, sin_sb)):
                for e in range(2):
                    factor = -1.0 if (g, e) == (1, 0) else 1.0
                    nc.gpsimd.tensor_scalar(
                        out=view[:, :, g, :, e],
                        in0=src[:, i0 : i0 + I // 2, :],
                        scalar1=factor,
                        scalar2=0.0,
                        op0=MULT,
                        op1=ADD,
                    )

        def permute(dst, src):
            nc.vector.tensor_copy(
                out=dst.rearrange("p (t m) -> p t m", t=4), in_=src.rearrange("p (m t) -> p t m", t=4)
            )

        xw, xt, xg, xq, xs, pc, cg, cq, cs, pr, ab, kt, vt, pu = [{} for j in range(14)]

        def x_source(n):
            b, i, w = units[n]
            if b > 0:
                return [xb_1, xb_2, xb_3][b - 1][:, i * E : (i + w) * E]
            return xb_first[:, i * E : (i + w) * E] if i < 2 else xb_rest[:, (i - 2) * E : (i - 2 + w) * E]

        def widen(n):
            w = units[n][2]
            xw[n] = work.tile([P, 2 * E], BF16, name="xw", bufs=4)
            copy = nc.scalar.copy if n in (1, 2, 3) else nc.vector.tensor_copy
            copy(out=xw[n][:, 0 : w * E], in_=x_source(n).bitcast(FP8))

        def turn(n):
            w = units[n][2]
            xt[n] = ps_x.tile([P, 2, 2 * P], F32, name="xt")
            words = xw[n][:].bitcast(F32)
            for j in range(w):
                for u in range(2):
                    nc.tensor.transpose(
                        xt[n][:, u, j * P : (j + 1) * P], words[:, j * 256 + u : (j + 1) * 256 : 2], ident[:]
                    )

        def scale_x(n):
            r = units[n][2] * P
            xg[n] = work.tile([P, 2 * P, 4], BF16, name="xg", align_bytes=64)
            nc.vector.tensor_tensor(
                out=xg[n][:, 0:r, :].rearrange("p r (u e) -> p r u e", e=2),
                in0=xt[n][:].bitcast(BF16).rearrange("p u (r e) -> p r u e", e=2)[:, 0:r],
                in1=xsc[:].unsqueeze(1).to_broadcast([P, r, 2, 2]),
                op=MULT,
            )

        def quant_x(n):
            r = units[n][2] * P
            xq[n] = work.tile([P, 2 * P], U32, name="xq", align_bytes=64)
            xs[n] = work.tile([P, 2 * P], U8, name="xs", align_bytes=64)
            nc.vector.quantize_mx(
                out=xq[n][:, 0:r].bitcast(FP8X4),
                scales=xs[n][:, 0:r],
                in_=xg[n][:, 0:r, :].rearrange("p r t -> p (r t)"),
            )

        def latent(n):
            pc[n] = []
            for j in range(units[n][2]):
                acc = ps_c.tile([P, 4, P], F32, name="pc")
                pc[n].append(acc)
                for t in range(4):
                    nc.tensor.matmul_mx(
                        out=acc[:, t, :],
                        lhsT=wd[:, t * P : (t + 1) * P].bitcast(FP8X4),
                        lhsT_scale=wd_s[:, t * P : (t + 1) * P],
                        rhs=xq[n][:, j * P : (j + 1) * P].bitcast(FP8X4),
                        rhs_scale=xs[n][:, j * P : (j + 1) * P],
                        start=True,
                        stop=True,
                    )

        def rope_key(n):
            pr[n] = ps_r.tile([P, 2, 2 * RD], F32, name="pr")
            for j in range(units[n][2]):
                nc.tensor.matmul_mx(
                    out=pr[n][:, j, :],
                    lhsT=xq[n][:, j * P : (j + 1) * P].bitcast(FP8X4),
                    lhsT_scale=xs[n][:, j * P : (j + 1) * P],
                    rhs=wd_raw[:, RK:].bitcast(FP8X4),
                    rhs_scale=wd_s_raw[:, RK:],
                    start=True,
                    stop=True,
                )

        def latent_out(n):
            cg[n] = work.tile([P, 2 * P, 4], BF16, name="cg", align_bytes=64)
            for j in range(units[n][2]):
                nc.scalar.copy(out=cg[n][:, j * P : (j + 1) * P, :], in_=pc[n][j][:].rearrange("p t r -> p r t"))

        def quant_c(n):
            r = units[n][2] * P
            cq[n] = work.tile([P, 2 * P], U32, name="cq", align_bytes=64)
            cs[n] = work.tile([P, 2 * P], U8, name="cs", align_bytes=64)
            nc.vector.quantize_mx(
                out=cq[n][:, 0:r].bitcast(FP8X4),
                scales=cs[n][:, 0:r],
                in_=cg[n][:, 0:r, :].rearrange("p r t -> p (r t)"),
            )

        def rotate(n):
            b, i, w = units[n]
            tab, i0 = (tab_a, 0) if i < I // 2 else (tab_b, I // 2)
            ab[n] = work.tile([P, 2, 2, RD], F32, name="ab")
            nc.vector.tensor_tensor(
                out=ab[n][:, 0:w],
                in0=pr[n][:, 0:w, :].rearrange("p w (g c) -> p w g c", g=2),
                in1=tab[:, i - i0 : i - i0 + w],
                op=MULT,
            )

        def rotate_sum(n):
            w = units[n][2]
            nc.vector.tensor_tensor(
                out=kt[n][:, 0:w, 0, DH:], in0=ab[n][:, 0:w, 0, :], in1=ab[n][:, 0:w, 1, :], op=ADD
            )

        def spread(n):
            w = units[n][2]
            out = kt[n][:, 0:w, 1:, DH:]
            src = kt[n][:, 0:w, 0:1, DH:].to_broadcast([P, w, H - 1, RD])
            if n == last:
                nc.vector.tensor_copy(out=out, in_=src)
            else:
                nc.gpsimd.tensor_scalar(out=out, in0=src, scalar1=1.0, scalar2=0.0, op0=MULT, op1=ADD)

        def new_out(n):
            kt[n] = outs.tile([P, 2, H, DV], F32, name="kt")
            vt[n] = outs.tile([P, 2, H, DV], F32, name="vt")

        def expand(n, j):
            for g in range(2):
                acc = ps_u.tile([P, 2, UP], F32, name="pu")
                pu[n, j, g] = acc
                cols = slice(g * 2 * UP, (g + 1) * 2 * UP)
                nc.tensor.matmul_mx(
                    out=acc[:].rearrange("p h c -> p (h c)"),
                    lhsT=cq[n][:, j * P : (j + 1) * P].bitcast(FP8X4),
                    lhsT_scale=cs[n][:, j * P : (j + 1) * P],
                    rhs=wu[:, cols].bitcast(FP8X4),
                    rhs_scale=wu_s[:, cols],
                    start=True,
                    stop=True,
                )

        def v_out_copy(n, j, g, copy):
            copy(out=vt[n][:, j, 2 * g : 2 * g + 2, :], in_=pu[n, j, g][:, :, DH:])

        def k_out_copy(n, j, g, copy):
            copy(out=kt[n][:, j, 2 * g : 2 * g + 2, 0:DH], in_=pu[n, j, g][:, :, 0:DH])

        def expand_out(n, j):
            for g in range(2):
                copy = nc.vector.tensor_copy if n in (0, last) and g == 1 else nc.scalar.copy
                v_out_copy(n, j, g, copy)
                k_out_copy(n, j, g, copy)

        def store(n):
            b, i, w = units[n]
            for hbm, sb in ((v_out, vt[n]), (k_out, kt[n])):
                nc.sync.dma_start(
                    out=hbm[b].rearrange("(p i) h d -> p i (h d)", i=I)[:, i : i + w, :],
                    in_=sb[:, 0:w].rearrange("p w h d -> p w (h d)"),
                )

        src = wd_raw[:, RK : RK + RD].bitcast(I32).rearrange("p (j e) -> p j e", e=2)
        dst = wd_raw[:, RK + RD :].bitcast(I32).rearrange("p (j e) -> p j e", e=2)
        src_s = wd_s_raw[:, RK : RK + RD].rearrange("p (j e) -> p j e", e=2)
        dst_s = wd_s_raw[:, RK + RD :].rearrange("p (j e) -> p j e", e=2)
        for e in range(2):
            nc.gpsimd.tensor_copy(out=dst[:, :, e], in_=src[:, :, 1 - e])
        for e in range(2):
            nc.gpsimd.tensor_copy(out=dst_s[:, :, e], in_=src_s[:, :, 1 - e])
        tables(tab_a, 0)

        for m in range(4):
            widen(m)
        for n in range(-4, last + 1):
            if n >= 0:
                new_out(n)
                quant_c(n)
                expand(n, 0)
                if n + 4 <= last:
                    widen(n + 4)
                rotate(n)
            if n == -3:
                permute(wd[:].bitcast(I32), wd_raw[:, 0:RK].bitcast(I32))
            if n == -2:
                permute(wd_s[:], wd_s_raw[:, 0:RK])
            if 0 <= n + 2 <= last:
                quant_x(n + 2)
            if n >= 0:
                expand_out(n, 0)
            if 0 <= n + 2 <= last:
                latent(n + 2)
            if n >= 0 and units[n][2] == 2:
                expand(n, 1)
            if 0 <= n + 2 <= last:
                latent_out(n + 2)
            if 0 <= n + 1 <= last:
                rope_key(n + 1)
            if n + 4 <= last:
                turn(n + 4)
            if n >= 0:
                rotate_sum(n)
                spread(n)
            if n == 0:
                tables(tab_b, I // 2)
            if 0 <= n + 3 <= last:
                scale_x(n + 3)
            if n >= 0:
                if units[n][2] == 2:
                    expand_out(n, 1)
                store(n)
